import numpy as np
import ml_dtypes


def mxq(x, axis, fmt="e4m3"):
    dtype, down = {"e4m3": (ml_dtypes.float8_e4m3fn, 7), "e5m2": (ml_dtypes.float8_e5m2, 14)}[fmt]
    v = np.moveaxis(np.asarray(x, np.float32).astype(ml_dtypes.bfloat16).astype(np.float64), axis, -1)
    blocks = v.reshape(v.shape[:-1] + (-1, 32))
    amax = np.abs(blocks).max(-1, keepdims=True)
    byte = np.maximum(np.where(amax > 0, np.frexp(amax)[1] - 1 + 127, 0) - down, 1)
    scale = np.exp2(byte - 127.0)
    codes = (blocks / scale).astype(np.float32).astype(dtype).astype(np.float64)
    return np.moveaxis((codes * scale).reshape(v.shape), -1, axis)


WIDE = False


def mx_kscale(k):
    if not WIDE:
        return np.ones(k)
    levels = np.array([10, -10, 5, -5, 0])
    a = np.random.permutation(np.resize(levels, k // 512 * 4)).reshape(k // 512, 4)
    idx = np.arange(k)
    return np.exp2(a[idx // 512, idx % 128 // 32])


BF16 = ml_dtypes.bfloat16


def bf(x):
    return np.asarray(x, np.float32).astype(BF16)


def f64(x):
    return np.asarray(x).astype(np.float64)


S, E, C, HD, HP = 2048, 768, 256, 1024, 1024
R = 2 * HP


def sigmoid(v):
    return 1.0 / (1.0 + np.exp(-v))


def setup_inputs():
    s, t = mx_kscale(R), mx_kscale(HD)
    return {"r": bf(np.abs(np.random.standard_normal((C, R))) * 0.5 * s),
            "psi_w1": bf(np.random.standard_normal((HD, R)) * 2.0 / np.sqrt(R) / s * t[:, None]),
            "psi_b1": bf(np.random.standard_normal(HD) * 0.3 * t),
            "w_dw": bf(np.random.standard_normal((E, HD)) * 1.5 / np.sqrt(HD) / t),
            "b_dw": bf(np.random.standard_normal(E) * 0.3),
            "w_gate": bf(np.random.standard_normal((E, HD)) * 1.5 / np.sqrt(HD) / t),
            "b_gate": bf(np.random.standard_normal(E) * 0.3),
            "W0": bf(np.random.standard_normal(E) * 0.1)}


def reference(r, psi_w1, psi_b1, w_dw, b_dw, w_gate, b_gate, W0):
    hid = np.maximum((mxq(f64(r), 1, "e4m3") @ mxq(f64(psi_w1), 1, "e4m3").T) + f64(psi_b1), 0.0)
    hq = mxq(hid, 1, "e4m3")
    dW = (hq @ mxq(f64(w_dw), 1, "e4m3").T) + f64(b_dw)
    gate = sigmoid((hq @ mxq(f64(w_gate), 1, "e4m3").T) + f64(b_gate))
    return f64(W0)[None, :] + gate * dW

@@ -1,0 +1,301 @@
+from contextlib import ExitStack
+
+import concourse.mybir as mybir
+from concourse.masks import make_identity
+
+F32 = mybir.dt.float32
+BF16 = mybir.dt.bfloat16
+U32 = mybir.dt.uint32
+U8 = mybir.dt.uint8
+FP8X4 = mybir.dt.float8_e4m3fn_x4
+ACT = mybir.ActivationFunctionType
+ALU = mybir.AluOpType
+
+P = 128
+C, R, HD, E = 256, 2048, 1024, 768
+FLOPS = 2 * C * R * HD + 2 * 2 * C * HD * E
+
+PIN = False
+V_BANKS = {0: (3,), 1: (3,), 2: (3,), 3: (3,), 4: (3,), 5: (), 6: (), 7: (1, 3)}
+
+
+def tile_metalinearheadml_pb_kernel(tc, r, psi_w1, psi_b1, w_dw, b_dw, w_gate, b_gate, W0, out):
+    nc = tc.nc
+    with ExitStack() as ctx:
+        keep = ctx.enter_context(tc.tile_pool(name="keep", bufs=1))
+        stage = ctx.enter_context(tc.tile_pool(name="stage", bufs=3))
+        tp_pool = ctx.enter_context(tc.psum_pool(name="tp_pool", bufs=4))
+        acc_pool = ctx.enter_context(tc.psum_pool(name="acc_pool", bufs=4))
+        if PIN:
+            ctx.enter_context(tc.manual_schedule())
+
+        vec_in = keep.tile([P, 256], BF16, name="vec_in")
+        nc.vector.memset(vec_in[:], 0.0)
+        warm = keep.tile([P, 1], F32, name="warm")
+        nc.vector.memset(warm[:], 0.0)
+        warm2 = keep.tile([P, 1], F32, name="warm2")
+        nc.scalar.dma_start(out=vec_in[0:4, :], in_=psi_b1.rearrange("(a w) -> a w", a=4))
+        nc.scalar.dma_start(out=vec_in[4:7, :], in_=b_dw.rearrange("(a w) -> a w", a=3))
+        nc.scalar.dma_start(out=vec_in[7:10, :], in_=b_gate.rearrange("(a w) -> a w", a=3))
+        nc.scalar.dma_start(out=vec_in[10:13, :], in_=W0.rearrange("(a w) -> a w", a=3))
+        nc.scalar.activation(out=warm2[:], in_=warm[:], func=ACT.Sigmoid)
+        ident_f = keep.tile([P, P], F32, name="ident_f")
+        make_identity(nc, ident_f[:])
+        ident_b = keep.tile([P, P], BF16, name="ident_b")
+        make_identity(nc, ident_b[:])
+
+        r_sb = keep.tile([P, 2 * R], BF16, name="r_sb")
+        r_dram = r.rearrange("(a p) k -> p a k", a=2)
+        r_view = r_sb[:].rearrange("p (a k) -> p a k", a=2)
+        for h in range(2):
+            nc.sync.dma_start(out=r_view[:, :, 1024 * h : 1024 * h + 1024], in_=r_dram[:, :, 1024 * h : 1024 * h + 1024])
+        psi_dram = psi_w1.rearrange("(a p e) k -> a p (e k)", a=4, e=2)
+        psi_sb = []
+        for a in range(4):
+            t = keep.tile([P, 2 * R], BF16, name="psi_sb%d" % a)
+            nc.sync.dma_start(out=t[:], in_=psi_dram[a])
+            psi_sb.append(t)
+        dw_dram = w_dw.rearrange("(j p e) k -> j p (e k)", j=3, e=2)
+        gt_dram = w_gate.rearrange("(j p e) k -> j p (e k)", j=3, e=2)
+        w_sb = []
+        for j in range(3):
+            td = keep.tile([P, 2 * HD], BF16, name="dw_sb%d" % j)
+            nc.sync.dma_start(out=td[:], in_=dw_dram[j])
+            tg = keep.tile([P, 2 * HD], BF16, name="gt_sb%d" % j)
+            nc.sync.dma_start(out=tg[:], in_=gt_dram[j])
+            w_sb.append((td, tg))
+
+        codes = [keep.tile([P, 1024], U32, name="codes%d" % n, align_bytes=64) for n in range(8)]
+        planes = [keep.tile([P, 1024], U8, name="planes%d" % n, align_bytes=64) for n in range(8)]
+        groups = {}
+        banks = {}
+
+        def slices_of(n, b):
+            if n == 0:
+                src = r_sb[:].bitcast(F32)
+                return [src[:, a * 1024 + 256 * b + 128 * u : a * 1024 + 256 * b + 128 * u + 128] for u in range(2) for a in range(2)]
+            if n <= 4:
+                src = psi_sb[n - 1][:].bitcast(F32)
+                base = 512 * b
+            else:
+                src = w_sb[n - 5][b // 2][:].bitcast(F32)
+                base = 512 * (b % 2)
+            return [src[:, base + 128 * i : base + 128 * i + 128] for i in range(4)]
+
+        def transposes(n, bs=(0, 1, 2, 3)):
+            for b in bs:
+                tp = tp_pool.tile([P, 512], F32, name="tp", tag="tp")
+                for i, s in enumerate(slices_of(n, b)):
+                    nc.tensor.transpose(tp[:, 128 * i : 128 * i + 128], s, ident_f[:])
+                banks[(n, b)] = tp
+
+        def empty(n, bs=(0, 1, 2, 3)):
+            if n not in groups:
+                groups[n] = stage.tile([P, 4096], BF16, name="grp", tag="grp", align_bytes=64)
+            gw = groups[n][:].bitcast(F32)
+            for b in bs:
+                tp = banks[(n, b)]
+                dst = gw[:, 512 * b : 512 * b + 512]
+                if n == 0:
+                    o = dst.rearrange("q (c u) -> q c u", u=2)
+                    i = tp[:].rearrange("q (u c) -> q c u", u=2)
+                else:
+                    o = dst.rearrange("q (g m u) -> q g m u", g=2, u=2)
+                    i = tp[:].rearrange("q (g u m) -> q g m u", g=2, u=2)
+                if b in V_BANKS[n]:
+                    nc.vector.tensor_copy(out=o, in_=i)
+                else:
+                    nc.scalar.copy(out=o, in_=i)
+
+        def quantise(n, lo, hi):
+            nc.vector.quantize_mx(
+                out=codes[n][:, 256 * lo : 256 * hi].bitcast(FP8X4),
+                scales=planes[n][:, 256 * lo : 256 * hi],
+                in_=groups[n][:, 1024 * lo : 1024 * hi],
+            )
+
+        vec_w = keep.tile([P, 16], F32, name="vec_w")
+        vec_f = keep.tile([P, 32], F32, name="vec_f")
+        w0_b = keep.tile([P, E], F32, name="w0_b")
+
+        def vec_prep():
+            tpv = tp_pool.tile([P, 512], F32, name="tpv", tag="tp")
+            nc.tensor.transpose(tpv[:, 0:128], vec_in[:].bitcast(F32), ident_f[:])
+            nc.vector.tensor_copy(out=vec_w[:], in_=tpv[:, 0:16])
+            nc.vector.tensor_copy(out=vec_f[:], in_=vec_w[:].bitcast(BF16))
+
+        def w0_prep():
+            vb = vec_w[:].bitcast(BF16)
+            for half, js in ((0, (0, 1)), (1, (2,))):
+                wps = acc_pool.tile([P, 512], F32, name="wps", tag="acc")
+                for jj, j in enumerate(js):
+                    for e in range(2):
+                        col = 2 * (10 + j) + e
+                        nc.tensor.matmul(
+                            wps[:, (jj * 2 + e) * 128 : (jj * 2 + e) * 128 + 128],
+                            lhsT=vb[:, col : col + 1].to_broadcast([P, P]),
+                            rhs=ident_b[:],
+                            start=True,
+                            stop=True,
+                        )
+                w = 256 * len(js)
+                nc.vector.tensor_copy(
+                    out=w0_b[:, 512 * half : 512 * half + w].rearrange("c (j p e) -> c j p e", p=128, e=2),
+                    in_=wps[:, 0:w].rearrange("c (j e p) -> c j p e", p=128, e=2),
+                )
+
+        hbf = [keep.tile([P, 1024], BF16, name="hbf%d" % g) for g in range(2)]
+        grp_h = [keep.tile([P, 1024], BF16, name="grp_h%d" % g, align_bytes=64) for g in range(2)]
+        codes_h = [keep.tile([P, 256], U32, name="codes_h%d" % g, align_bytes=64) for g in range(2)]
+        planes_h = [keep.tile([P, 256], U8, name="planes_h%d" % g, align_bytes=64) for g in range(2)]
+        accs = {}
+
+        def mm_hidden(n):
+            acc = acc_pool.tile([P, 512], F32, name="acc1", tag="acc")
+            for e in range(2):
+                for g in range(4):
+                    cols = slice((e * 4 + g) * 128, (e * 4 + g) * 128 + 128)
+                    rc = slice(256 * g, 256 * g + 256)
+                    nc.tensor.matmul_mx(
+                        out=acc[:, 256 * e : 256 * e + 256],
+                        lhsT=codes[n][:, cols].bitcast(FP8X4),
+                        lhsT_scale=planes[n][:, cols],
+                        rhs=codes[0][:, rc].bitcast(FP8X4),
+                        rhs_scale=planes[0][:, rc],
+                        start=(g == 0),
+                        stop=(g == 3),
+                    )
+            accs[n] = acc
+
+        def relu_hidden(n):
+            a = n - 1
+            g2, u2 = a // 2, a % 2
+            acc = accs[n]
+            for e in range(2):
+                t = 2 * u2 + e
+                nc.scalar.activation(
+                    out=hbf[g2][:, 256 * t : 256 * t + 256],
+                    in_=acc[:, 256 * e : 256 * e + 256],
+                    func=ACT.Relu,
+                    bias=vec_f[:, 2 * a + e : 2 * a + e + 1],
+                )
+
+        def regroup_hidden(g2):
+            nc.vector.tensor_copy(
+                out=grp_h[g2][:].rearrange("p (c t) -> p c t", t=4),
+                in_=hbf[g2][:].rearrange("p (t c) -> p c t", t=4),
+            )
+
+        def quantise_hidden(g2):
+            nc.vector.quantize_mx(out=codes_h[g2][:].bitcast(FP8X4), scales=planes_h[g2][:], in_=grp_h[g2][:])
+
+        out_sb = keep.tile([P, 2 * E], F32, name="out_sb")
+        out_view = out_sb[:].rearrange("c (a x) -> c a x", a=2)
+        out_dram = out.rearrange("(a c) x -> c a x", a=2)
+        xs = {}
+
+        def mm_out(n, es=(0, 1)):
+            if n not in accs:
+                acc_g = acc_pool.tile([P, 512], F32, name="acc_g", tag="acc")
+                acc_d = acc_pool.tile([P, 512], F32, name="acc_d", tag="acc")
+                accs[n] = (acc_d, acc_g)
+            for e in es:
+                for mat in (1, 0):
+                    for g2 in range(2):
+                        cols = slice(((mat * 2 + e) * 2 + g2) * 128, ((mat * 2 + e) * 2 + g2) * 128 + 128)
+                        nc.tensor.matmul_mx(
+                            out=accs[n][mat][:, 256 * e : 256 * e + 256],
+                            lhsT=codes[n][:, cols].bitcast(FP8X4),
+                            lhsT_scale=planes[n][:, cols],
+                            rhs=codes_h[g2][:].bitcast(FP8X4),
+                            rhs_scale=planes_h[g2][:],
+                            start=(g2 == 0),
+                            stop=(g2 == 1),
+                        )
+
+        def gate_out(n, es=(0, 1)):
+            j = n - 5
+            if n not in xs:
+                gate = stage.tile([P, 512], F32, name="gate", tag="gate")
+                x = stage.tile([P, 512], F32, name="x", tag="x")
+                xs[n] = (gate, x)
+            gate, x = xs[n]
+            acc_d, acc_g = accs[n]
+            for e in es:
+                cs = slice(256 * e, 256 * e + 256)
+                nc.scalar.activation(
+                    out=gate[:, cs], in_=acc_g[:, cs], func=ACT.Sigmoid, bias=vec_f[:, 2 * (7 + j) + e : 2 * (7 + j) + e + 1]
+                )
+                nc.vector.scalar_tensor_tensor(
+                    out=x[:, cs],
+                    in0=acc_d[:, cs],
+                    scalar=vec_f[:, 2 * (4 + j) + e : 2 * (4 + j) + e + 1],
+                    in1=gate[:, cs],
+                    op0=ALU.add,
+                    op1=ALU.mult,
+                )
+
+        fins = {}
+
+        def back(n):
+            x = xs[n][1]
+            fin = tp_pool.tile([P, 512], F32, name="fin", tag="tp")
+            for a in range(2):
+                for e in range(2):
+                    nc.tensor.transpose(
+                        fin[:, (a * 2 + e) * 128 : (a * 2 + e) * 128 + 128], x[:, 256 * e + 128 * a : 256 * e + 128 * a + 128], ident_f[:]
+                    )
+            fins[n] = fin
+
+        def finish(n):
+            j = n - 5
+            xc = slice(256 * j, 256 * j + 256)
+            nc.vector.tensor_tensor(
+                out=out_view[:, :, xc].rearrange("c a (p e) -> c a p e", e=2),
+                in0=fins[n][:].rearrange("c (a e p) -> c a p e", a=2, e=2),
+                in1=w0_b[:, xc].rearrange("c (p e) -> c p e", e=2).unsqueeze(1).to_broadcast([P, 2, 128, 2]),
+                op=ALU.add,
+            )
+            nc.sync.dma_start(out=out_dram[:, :, xc], in_=out_view[:, :, xc])
+
+        transposes(0)
+        empty(0)
+        quantise(0, 0, 2)
+        quantise(0, 2, 4)
+        vec_prep()
+        transposes(1)
+        empty(1)
+        quantise(1, 0, 2)
+        quantise(1, 2, 4)
+        w0_prep()
+        for n in range(2, 8):
+            transposes(n)
+            if n - 1 <= 4:
+                mm_hidden(n - 1)
+            else:
+                mm_out(n - 1)
+            if n - 2 >= 5:
+                back(n - 2)
+            empty(n)
+            if n - 1 <= 4:
+                relu_hidden(n - 1)
+                if n - 1 == 2:
+                    regroup_hidden(0)
+                if n - 1 == 4:
+                    regroup_hidden(1)
+            else:
+                gate_out(n - 1)
+            quantise(n, 0, 2)
+            if n - 1 == 2:
+                quantise_hidden(0)
+            if n - 1 == 4:
+                quantise_hidden(1)
+            quantise(n, 2, 4)
+            if n - 2 >= 5:
+                finish(n - 2)
+        mm_out(7)
+        back(6)
+        gate_out(7)
+        finish(6)
+        back(7)
+        finish(7)

@@ -15,8 +15,8 @@ P = 128
 C, R, HD, E = 256, 2048, 1024, 768
 FLOPS = 2 * C * R * HD + 2 * 2 * C * HD * E
 
-PIN = False
-V_BANKS = {0: (3,), 1: (3,), 2: (3,), 3: (3,), 4: (3,), 5: (), 6: (), 7: (1, 3)}
+PIN = True
+V_BANKS = {0: (1, 3), 1: (3,), 2: (3,), 3: (3,), 4: (3,), 5: (3,), 6: (), 7: ()}
 
 
 def tile_metalinearheadml_pb_kernel(tc, r, psi_w1, psi_b1, w_dw, b_dw, w_gate, b_gate, W0, out):
@@ -24,8 +24,7 @@ def tile_metalinearheadml_pb_kernel(tc, r, psi_w1, psi_b1, w_dw, b_dw, w_gate, b
     with ExitStack() as ctx:
         keep = ctx.enter_context(tc.tile_pool(name="keep", bufs=1))
         stage = ctx.enter_context(tc.tile_pool(name="stage", bufs=3))
-        tp_pool = ctx.enter_context(tc.psum_pool(name="tp_pool", bufs=4))
-        acc_pool = ctx.enter_context(tc.psum_pool(name="acc_pool", bufs=4))
+        ps_pool = ctx.enter_context(tc.psum_pool(name="ps_pool", bufs=8))
         if PIN:
             ctx.enter_context(tc.manual_schedule())
 
@@ -49,11 +48,12 @@ def tile_metalinearheadml_pb_kernel(tc, r, psi_w1, psi_b1, w_dw, b_dw, w_gate, b
         r_view = r_sb[:].rearrange("p (a k) -> p a k", a=2)
         for h in range(2):
             nc.sync.dma_start(out=r_view[:, :, 1024 * h : 1024 * h + 1024], in_=r_dram[:, :, 1024 * h : 1024 * h + 1024])
-        psi_dram = psi_w1.rearrange("(a p e) k -> a p (e k)", a=4, e=2)
+        psi_dram = psi_w1.rearrange("(a p e) k -> a e p k", a=4, e=2)
         psi_sb = []
         for a in range(4):
             t = keep.tile([P, 2 * R], BF16, name="psi_sb%d" % a)
-            nc.sync.dma_start(out=t[:], in_=psi_dram[a])
+            for e in range(2):
+                nc.sync.dma_start(out=t[:, R * e : R * e + R], in_=psi_dram[a, e])
             psi_sb.append(t)
         dw_dram = w_dw.rearrange("(j p e) k -> j p (e k)", j=3, e=2)
         gt_dram = w_gate.rearrange("(j p e) k -> j p (e k)", j=3, e=2)
@@ -84,7 +84,7 @@ def tile_metalinearheadml_pb_kernel(tc, r, psi_w1, psi_b1, w_dw, b_dw, w_gate, b
 
         def transposes(n, bs=(0, 1, 2, 3)):
             for b in bs:
-                tp = tp_pool.tile([P, 512], F32, name="tp", tag="tp")
+                tp = ps_pool.tile([P, 512], F32, name="tp", tag="ps")
                 for i, s in enumerate(slices_of(n, b)):
                     nc.tensor.transpose(tp[:, 128 * i : 128 * i + 128], s, ident_f[:])
                 banks[(n, b)] = tp
@@ -119,15 +119,18 @@ def tile_metalinearheadml_pb_kernel(tc, r, psi_w1, psi_b1, w_dw, b_dw, w_gate, b
         w0_b = keep.tile([P, E], F32, name="w0_b")
 
         def vec_prep():
-            tpv = tp_pool.tile([P, 512], F32, name="tpv", tag="tp")
+            tpv = ps_pool.tile([P, 512], F32, name="tpv", tag="ps")
             nc.tensor.transpose(tpv[:, 0:128], vec_in[:].bitcast(F32), ident_f[:])
             nc.vector.tensor_copy(out=vec_w[:], in_=tpv[:, 0:16])
             nc.vector.tensor_copy(out=vec_f[:], in_=vec_w[:].bitcast(BF16))
 
-        def w0_prep():
+        w0_ps = []
+
+        def w0_mm():
             vb = vec_w[:].bitcast(BF16)
             for half, js in ((0, (0, 1)), (1, (2,))):
-                wps = acc_pool.tile([P, 512], F32, name="wps", tag="acc")
+                wps = ps_pool.tile([P, 512], F32, name="wps", tag="ps")
+                w0_ps.append(wps)
                 for jj, j in enumerate(js):
                     for e in range(2):
                         col = 2 * (10 + j) + e
@@ -138,6 +141,10 @@ def tile_metalinearheadml_pb_kernel(tc, r, psi_w1, psi_b1, w_dw, b_dw, w_gate, b
                             start=True,
                             stop=True,
                         )
+
+        def w0_out():
+            for half, js in ((0, (0, 1)), (1, (2,))):
+                wps = w0_ps[half]
                 w = 256 * len(js)
                 nc.vector.tensor_copy(
                     out=w0_b[:, 512 * half : 512 * half + w].rearrange("c (j p e) -> c j p e", p=128, e=2),
@@ -151,7 +158,7 @@ def tile_metalinearheadml_pb_kernel(tc, r, psi_w1, psi_b1, w_dw, b_dw, w_gate, b
         accs = {}
 
         def mm_hidden(n):
-            acc = acc_pool.tile([P, 512], F32, name="acc1", tag="acc")
+            acc = ps_pool.tile([P, 512], F32, name="acc1", tag="ps")
             for e in range(2):
                 for g in range(4):
                     cols = slice((e * 4 + g) * 128, (e * 4 + g) * 128 + 128)
@@ -196,11 +203,11 @@ def tile_metalinearheadml_pb_kernel(tc, r, psi_w1, psi_b1, w_dw, b_dw, w_gate, b
 
         def mm_out(n, es=(0, 1)):
             if n not in accs:
-                acc_g = acc_pool.tile([P, 512], F32, name="acc_g", tag="acc")
-                acc_d = acc_pool.tile([P, 512], F32, name="acc_d", tag="acc")
+                acc_g = ps_pool.tile([P, 512], F32, name="acc_g", tag="ps")
+                acc_d = ps_pool.tile([P, 512], F32, name="acc_d", tag="ps")
                 accs[n] = (acc_d, acc_g)
-            for e in es:
-                for mat in (1, 0):
+            for mat in (1, 0):
+                for e in es:
                     for g2 in range(2):
                         cols = slice(((mat * 2 + e) * 2 + g2) * 128, ((mat * 2 + e) * 2 + g2) * 128 + 128)
                         nc.tensor.matmul_mx(
@@ -226,6 +233,8 @@ def tile_metalinearheadml_pb_kernel(tc, r, psi_w1, psi_b1, w_dw, b_dw, w_gate, b
                 nc.scalar.activation(
                     out=gate[:, cs], in_=acc_g[:, cs], func=ACT.Sigmoid, bias=vec_f[:, 2 * (7 + j) + e : 2 * (7 + j) + e + 1]
                 )
+            for e in es:
+                cs = slice(256 * e, 256 * e + 256)
                 nc.vector.scalar_tensor_tensor(
                     out=x[:, cs],
                     in0=acc_d[:, cs],
@@ -239,7 +248,7 @@ def tile_metalinearheadml_pb_kernel(tc, r, psi_w1, psi_b1, w_dw, b_dw, w_gate, b
 
         def back(n):
             x = xs[n][1]
-            fin = tp_pool.tile([P, 512], F32, name="fin", tag="tp")
+            fin = ps_pool.tile([P, 512], F32, name="fin", tag="ps")
             for a in range(2):
                 for e in range(2):
                     nc.tensor.transpose(
@@ -258,43 +267,57 @@ def tile_metalinearheadml_pb_kernel(tc, r, psi_w1, psi_b1, w_dw, b_dw, w_gate, b
             )
             nc.sync.dma_start(out=out_dram[:, :, xc], in_=out_view[:, :, xc])
 
+        def quantise_all(n):
+            quantise(n, 0, 2)
+            quantise(n, 2, 4)
+
         transposes(0)
         empty(0)
-        quantise(0, 0, 2)
-        quantise(0, 2, 4)
         vec_prep()
         transposes(1)
+        quantise_all(0)
         empty(1)
-        quantise(1, 0, 2)
-        quantise(1, 2, 4)
-        w0_prep()
-        for n in range(2, 8):
-            transposes(n)
-            if n - 1 <= 4:
-                mm_hidden(n - 1)
-            else:
-                mm_out(n - 1)
-            if n - 2 >= 5:
-                back(n - 2)
-            empty(n)
-            if n - 1 <= 4:
-                relu_hidden(n - 1)
-                if n - 1 == 2:
-                    regroup_hidden(0)
-                if n - 1 == 4:
-                    regroup_hidden(1)
-            else:
-                gate_out(n - 1)
-            quantise(n, 0, 2)
-            if n - 1 == 2:
-                quantise_hidden(0)
-            if n - 1 == 4:
-                quantise_hidden(1)
-            quantise(n, 2, 4)
-            if n - 2 >= 5:
-                finish(n - 2)
+        w0_mm()
+        transposes(2)
+        quantise_all(1)
+        w0_out()
+        mm_hidden(1)
+        empty(2)
+        transposes(3)
+        quantise_all(2)
+        mm_hidden(2)
+        relu_hidden(1)
+        empty(3)
+        transposes(4)
+        quantise_all(3)
+        mm_hidden(3)
+        relu_hidden(2)
+        regroup_hidden(0)
+        quantise_hidden(0)
+        empty(4)
+        transposes(5)
+        quantise_all(4)
+        mm_hidden(4)
+        relu_hidden(3)
+        empty(5)
+        transposes(6)
+        quantise_all(5)
+        relu_hidden(4)
+        empty(6)
+        regroup_hidden(1)
+        quantise_hidden(1)
+        transposes(7)
+        quantise_all(6)
+        empty(7)
+        mm_out(5)
+        quantise_all(7)
+        gate_out(5)
+        mm_out(6)
+        gate_out(6)
         mm_out(7)
+        back(5)
         back(6)
+        finish(5)
         gate_out(7)
         finish(6)
         back(7)

@@ -43,11 +43,12 @@ def tile_metalinearheadml_pb_kernel(tc, r, psi_w1, psi_b1, w_dw, b_dw, w_gate, b
         ident_b = keep.tile([P, P], BF16, name="ident_b")
         make_identity(nc, ident_b[:])
 
-        r_sb = keep.tile([P, 2 * R], BF16, name="r_sb")
         r_dram = r.rearrange("(a p) k -> p a k", a=2)
-        r_view = r_sb[:].rearrange("p (a k) -> p a k", a=2)
+        r_sb = []
         for h in range(2):
-            nc.sync.dma_start(out=r_view[:, :, 1024 * h : 1024 * h + 1024], in_=r_dram[:, :, 1024 * h : 1024 * h + 1024])
+            t = keep.tile([P, R], BF16, name="r_sb%d" % h)
+            nc.sync.dma_start(out=t[:].rearrange("p (a k) -> p a k", a=2), in_=r_dram[:, :, 1024 * h : 1024 * h + 1024])
+            r_sb.append(t)
         psi_dram = psi_w1.rearrange("(a p e) k -> a e p k", a=4, e=2)
         psi_sb = []
         for a in range(4):
@@ -72,8 +73,9 @@ def tile_metalinearheadml_pb_kernel(tc, r, psi_w1, psi_b1, w_dw, b_dw, w_gate, b
 
         def slices_of(n, b):
             if n == 0:
-                src = r_sb[:].bitcast(F32)
-                return [src[:, a * 1024 + 256 * b + 128 * u : a * 1024 + 256 * b + 128 * u + 128] for u in range(2) for a in range(2)]
+                src = r_sb[b // 2][:].bitcast(F32)
+                base = 256 * (b % 2)
+                return [src[:, a * 512 + base + 128 * u : a * 512 + base + 128 * u + 128] for u in range(2) for a in range(2)]
             if n <= 4:
                 src = psi_sb[n - 1][:].bitcast(F32)
                 base = 512 * b
@@ -196,8 +198,7 @@ def tile_metalinearheadml_pb_kernel(tc, r, psi_w1, psi_b1, w_dw, b_dw, w_gate, b
         def quantise_hidden(g2):
             nc.vector.quantize_mx(out=codes_h[g2][:].bitcast(FP8X4), scales=planes_h[g2][:], in_=grp_h[g2][:])
 
-        out_sb = keep.tile([P, 2 * E], F32, name="out_sb")
-        out_view = out_sb[:].rearrange("c (a x) -> c a x", a=2)
+        out_sb = [keep.tile([P, 512], F32, name="out_sb%d" % j) for j in range(3)]
         out_dram = out.rearrange("(a c) x -> c a x", a=2)
         xs = {}
 
@@ -260,12 +261,12 @@ def tile_metalinearheadml_pb_kernel(tc, r, psi_w1, psi_b1, w_dw, b_dw, w_gate, b
             j = n - 5
             xc = slice(256 * j, 256 * j + 256)
             nc.vector.tensor_tensor(
-                out=out_view[:, :, xc].rearrange("c a (p e) -> c a p e", e=2),
+                out=out_sb[j][:].rearrange("c (a p e) -> c a p e", a=2, e=2),
                 in0=fins[n][:].rearrange("c (a e p) -> c a p e", a=2, e=2),
                 in1=w0_b[:, xc].rearrange("c (p e) -> c p e", e=2).unsqueeze(1).to_broadcast([P, 2, 128, 2]),
                 op=ALU.add,
             )
-            nc.sync.dma_start(out=out_dram[:, :, xc], in_=out_view[:, :, xc])
+            nc.sync.dma_start(out=out_dram[:, :, xc], in_=out_sb[j][:].rearrange("c (a x) -> c a x", a=2))
 
         def quantise_all(n):
             quantise(n, 0, 2)

@@ -16,7 +16,7 @@ C, R, HD, E = 256, 2048, 1024, 768
 FLOPS = 2 * C * R * HD + 2 * 2 * C * HD * E
 
 PIN = True
-V_BANKS = {0: (1, 3), 1: (3,), 2: (3,), 3: (3,), 4: (3,), 5: (3,), 6: (), 7: ()}
+V_BANKS = {0: (1, 3), 1: (3,), 2: (3,), 3: (3,), 4: (3,), 5: (3,), 6: (3,), 7: ()}
 
 
 def tile_metalinearheadml_pb_kernel(tc, r, psi_w1, psi_b1, w_dw, b_dw, w_gate, b_gate, W0, out):
@@ -161,12 +161,16 @@ def tile_metalinearheadml_pb_kernel(tc, r, psi_w1, psi_b1, w_dw, b_dw, w_gate, b
 
         def mm_hidden(n):
             acc = ps_pool.tile([P, 512], F32, name="acc1", tag="ps")
+            acc_b = acc
+            if n == 4:
+                acc_b = ps_pool.tile([P, 512], F32, name="acc1b", tag="ps")
+            accs[n] = (acc, acc_b)
             for e in range(2):
                 for g in range(4):
                     cols = slice((e * 4 + g) * 128, (e * 4 + g) * 128 + 128)
                     rc = slice(256 * g, 256 * g + 256)
                     nc.tensor.matmul_mx(
-                        out=acc[:, 256 * e : 256 * e + 256],
+                        out=accs[n][e][:, 256 * e : 256 * e + 256],
                         lhsT=codes[n][:, cols].bitcast(FP8X4),
                         lhsT_scale=planes[n][:, cols],
                         rhs=codes[0][:, rc].bitcast(FP8X4),
@@ -174,20 +178,28 @@ def tile_metalinearheadml_pb_kernel(tc, r, psi_w1, psi_b1, w_dw, b_dw, w_gate, b
                         start=(g == 0),
                         stop=(g == 3),
                     )
-            accs[n] = acc
 
         def relu_hidden(n):
             a = n - 1
             g2, u2 = a // 2, a % 2
-            acc = accs[n]
             for e in range(2):
                 t = 2 * u2 + e
-                nc.scalar.activation(
-                    out=hbf[g2][:, 256 * t : 256 * t + 256],
-                    in_=acc[:, 256 * e : 256 * e + 256],
-                    func=ACT.Relu,
-                    bias=vec_f[:, 2 * a + e : 2 * a + e + 1],
-                )
+                if n == 4 and e == 1:
+                    nc.vector.tensor_scalar(
+                        out=hbf[g2][:, 256 * t : 256 * t + 256],
+                        in0=accs[n][e][:, 256 * e : 256 * e + 256],
+                        scalar1=vec_f[:, 2 * a + e : 2 * a + e + 1],
+                        scalar2=0.0,
+                        op0=ALU.add,
+                        op1=ALU.max,
+                    )
+                else:
+                    nc.scalar.activation(
+                        out=hbf[g2][:, 256 * t : 256 * t + 256],
+                        in_=accs[n][e][:, 256 * e : 256 * e + 256],
+                        func=ACT.Relu,
+                        bias=vec_f[:, 2 * a + e : 2 * a + e + 1],
+                    )
 
         def regroup_hidden(g2):
             nc.vector.tensor_copy(
@@ -304,9 +316,9 @@ def tile_metalinearheadml_pb_kernel(tc, r, psi_w1, psi_b1, w_dw, b_dw, w_gate, b
         transposes(6)
         quantise_all(5)
         relu_hidden(4)
-        empty(6)
         regroup_hidden(1)
         quantise_hidden(1)
+        empty(6)
         transposes(7)
         quantise_all(6)
         empty(7)
@@ -318,8 +330,8 @@ def tile_metalinearheadml_pb_kernel(tc, r, psi_w1, psi_b1, w_dw, b_dw, w_gate, b
         mm_out(7)
         back(5)
         back(6)
-        finish(5)
         gate_out(7)
-        finish(6)
+        finish(5)
         back(7)
+        finish(6)
         finish(7)

@@ -28,6 +28,8 @@ def tile_metalinearheadml_pb_kernel(tc, r, psi_w1, psi_b1, w_dw, b_dw, w_gate, b
         if PIN:
             ctx.enter_context(tc.manual_schedule())
 
+        zf = keep.tile([P, P], F32, name="zf")
+        nc.vector.memset(zf[:], 0.0)
         vec_in = keep.tile([P, 256], BF16, name="vec_in")
         nc.vector.memset(vec_in[:], 0.0)
         warm = keep.tile([P, 1], F32, name="warm")
@@ -284,14 +286,27 @@ def tile_metalinearheadml_pb_kernel(tc, r, psi_w1, psi_b1, w_dw, b_dw, w_gate, b
             quantise(n, 0, 2)
             quantise(n, 2, 4)
 
-        transposes(0)
+        def dummies(k):
+            dm = ps_pool.tile([P, 512], F32, name="dm", tag="ps")
+            for i in range(k):
+                nc.tensor.matmul(dm[:, 0:128], lhsT=zf[:], rhs=zf[:], start=True, stop=True)
+
+        dummies(6)
+        transposes(0, (0, 1))
+        dummies(2)
+        transposes(0, (2, 3))
+        dummies(2)
         empty(0)
         vec_prep()
-        transposes(1)
+        transposes(1, (0, 1))
+        dummies(2)
+        transposes(1, (2, 3))
         quantise_all(0)
         empty(1)
         w0_mm()
-        transposes(2)
+        transposes(2, (0, 1))
+        dummies(2)
+        transposes(2, (2, 3))
         quantise_all(1)
         w0_out()
         mm_hidden(1)

@@ -28,8 +28,6 @@ def tile_metalinearheadml_pb_kernel(tc, r, psi_w1, psi_b1, w_dw, b_dw, w_gate, b
         if PIN:
             ctx.enter_context(tc.manual_schedule())
 
-        zf = keep.tile([P, P], F32, name="zf")
-        nc.vector.memset(zf[:], 0.0)
         vec_in = keep.tile([P, 256], BF16, name="vec_in")
         nc.vector.memset(vec_in[:], 0.0)
         warm = keep.tile([P, 1], F32, name="warm")
@@ -62,11 +60,11 @@ def tile_metalinearheadml_pb_kernel(tc, r, psi_w1, psi_b1, w_dw, b_dw, w_gate, b
         gt_dram = w_gate.rearrange("(j p e) k -> j p (e k)", j=3, e=2)
         w_sb = []
         for j in range(3):
-            td = keep.tile([P, 2 * HD], BF16, name="dw_sb%d" % j)
-            nc.sync.dma_start(out=td[:], in_=dw_dram[j])
             tg = keep.tile([P, 2 * HD], BF16, name="gt_sb%d" % j)
             nc.sync.dma_start(out=tg[:], in_=gt_dram[j])
-            w_sb.append((td, tg))
+            td = keep.tile([P, 2 * HD], BF16, name="dw_sb%d" % j)
+            nc.sync.dma_start(out=td[:], in_=dw_dram[j])
+            w_sb.append((tg, td))
 
         codes = [keep.tile([P, 1024], U32, name="codes%d" % n, align_bytes=64) for n in range(8)]
         planes = [keep.tile([P, 1024], U8, name="planes%d" % n, align_bytes=64) for n in range(8)]
@@ -205,8 +203,8 @@ def tile_metalinearheadml_pb_kernel(tc, r, psi_w1, psi_b1, w_dw, b_dw, w_gate, b
 
         def regroup_hidden(g2):
             nc.vector.tensor_copy(
-                out=grp_h[g2][:].rearrange("p (c t) -> p c t", t=4),
-                in_=hbf[g2][:].rearrange("p (t c) -> p c t", t=4),
+                out=grp_h[g2][:].rearrange("p (c i t) -> p c t i", i=4, t=4),
+                in_=hbf[g2][:].rearrange("p (t c i) -> p c t i", t=4, i=4),
             )
 
         def quantise_hidden(g2):
@@ -224,7 +222,8 @@ def tile_metalinearheadml_pb_kernel(tc, r, psi_w1, psi_b1, w_dw, b_dw, w_gate, b
             for mat in (1, 0):
                 for e in es:
                     for g2 in range(2):
-                        cols = slice(((mat * 2 + e) * 2 + g2) * 128, ((mat * 2 + e) * 2 + g2) * 128 + 128)
+                        bank = (1 - mat) * 2 + e
+                        cols = slice((bank * 2 + g2) * 128, (bank * 2 + g2) * 128 + 128)
                         nc.tensor.matmul_mx(
                             out=accs[n][mat][:, 256 * e : 256 * e + 256],
                             lhsT=codes[n][:, cols].bitcast(FP8X4),
@@ -286,27 +285,14 @@ def tile_metalinearheadml_pb_kernel(tc, r, psi_w1, psi_b1, w_dw, b_dw, w_gate, b
             quantise(n, 0, 2)
             quantise(n, 2, 4)
 
-        def dummies(k):
-            dm = ps_pool.tile([P, 512], F32, name="dm", tag="ps")
-            for i in range(k):
-                nc.tensor.matmul(dm[:, 0:128], lhsT=zf[:], rhs=zf[:], start=True, stop=True)
-
-        dummies(6)
-        transposes(0, (0, 1))
-        dummies(2)
-        transposes(0, (2, 3))
-        dummies(2)
+        transposes(0)
         empty(0)
         vec_prep()
-        transposes(1, (0, 1))
-        dummies(2)
-        transposes(1, (2, 3))
+        transposes(1)
         quantise_all(0)
         empty(1)
         w0_mm()
-        transposes(2, (0, 1))
-        dummies(2)
-        transposes(2, (2, 3))
+        transposes(2)
         quantise_all(1)
         w0_out()
         mm_hidden(1)
@@ -338,7 +324,9 @@ def tile_metalinearheadml_pb_kernel(tc, r, psi_w1, psi_b1, w_dw, b_dw, w_gate, b
         quantise_all(6)
         empty(7)
         mm_out(5)
-        quantise_all(7)
+        quantise(7, 0, 2)
+        quantise(7, 2, 3)
+        quantise(7, 3, 4)
         gate_out(5)
         mm_out(6)
         gate_out(6)

from contextlib import ExitStack

import concourse.mybir as mybir
from concourse.masks import make_identity

F32 = mybir.dt.float32
BF16 = mybir.dt.bfloat16
U32 = mybir.dt.uint32
U8 = mybir.dt.uint8
FP8X4 = mybir.dt.float8_e4m3fn_x4
ACT = mybir.ActivationFunctionType
ALU = mybir.AluOpType

P = 128
C, R, HD, E = 256, 2048, 1024, 768
FLOPS = 2 * C * R * HD + 2 * 2 * C * HD * E

PIN = True
V_BANKS = {0: (1, 3), 1: (3,), 2: (3,), 3: (3,), 4: (3,), 5: (3,), 6: (3,), 7: ()}


def tile_metalinearheadml_pb_kernel(tc, r, psi_w1, psi_b1, w_dw, b_dw, w_gate, b_gate, W0, out):
    nc = tc.nc
    with ExitStack() as ctx:
        keep = ctx.enter_context(tc.tile_pool(name="keep", bufs=1))
        stage = ctx.enter_context(tc.tile_pool(name="stage", bufs=3))
        ps_pool = ctx.enter_context(tc.psum_pool(name="ps_pool", bufs=8))
        if PIN:
            ctx.enter_context(tc.manual_schedule())

        vec_in = keep.tile([P, 256], BF16, name="vec_in")
        nc.vector.memset(vec_in[:], 0.0)
        warm = keep.tile([P, 1], F32, name="warm")
        nc.vector.memset(warm[:], 0.0)
        warm2 = keep.tile([P, 1], F32, name="warm2")
        nc.scalar.dma_start(out=vec_in[0:4, :], in_=psi_b1.rearrange("(a w) -> a w", a=4))
        nc.scalar.dma_start(out=vec_in[4:7, :], in_=b_dw.rearrange("(a w) -> a w", a=3))
        nc.scalar.dma_start(out=vec_in[7:10, :], in_=b_gate.rearrange("(a w) -> a w", a=3))
        nc.scalar.dma_start(out=vec_in[10:13, :], in_=W0.rearrange("(a w) -> a w", a=3))
        nc.scalar.activation(out=warm2[:], in_=warm[:], func=ACT.Sigmoid)
        ident_f = keep.tile([P, P], F32, name="ident_f")
        make_identity(nc, ident_f[:])
        ident_b = keep.tile([P, P], BF16, name="ident_b")
        make_identity(nc, ident_b[:])

        r_dram = r.rearrange("(a p) k -> p a k", a=2)
        r_sb = []
        for h in range(2):
            t = keep.tile([P, R], BF16, name="r_sb%d" % h)
            nc.sync.dma_start(out=t[:].rearrange("p (a k) -> p a k", a=2), in_=r_dram[:, :, 1024 * h : 1024 * h + 1024])
            r_sb.append(t)
        psi_dram = psi_w1.rearrange("(a p e) k -> a e p k", a=4, e=2)
        psi_sb = []
        for a in range(4):
            t = keep.tile([P, 2 * R], BF16, name="psi_sb%d" % a)
            for e in range(2):
                nc.sync.dma_start(out=t[:, R * e : R * e + R], in_=psi_dram[a, e])
            psi_sb.append(t)
        dw_dram = w_dw.rearrange("(j p e) k -> j p (e k)", j=3, e=2)
        gt_dram = w_gate.rearrange("(j p e) k -> j p (e k)", j=3, e=2)
        w_sb = []
        for j in range(3):
            tg = keep.tile([P, 2 * HD], BF16, name="gt_sb%d" % j)
            nc.sync.dma_start(out=tg[:], in_=gt_dram[j])
            td = keep.tile([P, 2 * HD], BF16, name="dw_sb%d" % j)
            nc.sync.dma_start(out=td[:], in_=dw_dram[j])
            w_sb.append((tg, td))

        codes = [keep.tile([P, 1024], U32, name="codes%d" % n, align_bytes=64) for n in range(8)]
        planes = [keep.tile([P, 1024], U8, name="planes%d" % n, align_bytes=64) for n in range(8)]
        groups = {}
        banks = {}

        def slices_of(n, b):
            if n == 0:
                src = r_sb[b // 2][:].bitcast(F32)
                base = 256 * (b % 2)
                return [src[:, a * 512 + base + 128 * u : a * 512 + base + 128 * u + 128] for u in range(2) for a in range(2)]
            if n <= 4:
                src = psi_sb[n - 1][:].bitcast(F32)
                base = 512 * b
            else:
                src = w_sb[n - 5][b // 2][:].bitcast(F32)
                base = 512 * (b % 2)
            return [src[:, base + 128 * i : base + 128 * i + 128] for i in range(4)]

        def transposes(n, bs=(0, 1, 2, 3)):
            for b in bs:
                tp = ps_pool.tile([P, 512], F32, name="tp", tag="ps")
                for i, s in enumerate(slices_of(n, b)):
                    nc.tensor.transpose(tp[:, 128 * i : 128 * i + 128], s, ident_f[:])
                banks[(n, b)] = tp

        def empty(n, bs=(0, 1, 2, 3)):
            if n not in groups:
                groups[n] = stage.tile([P, 4096], BF16, name="grp", tag="grp", align_bytes=64)
            gw = groups[n][:].bitcast(F32)
            for b in bs:
                tp = banks[(n, b)]
                dst = gw[:, 512 * b : 512 * b + 512]
                if n == 0:
                    o = dst.rearrange("q (c u) -> q c u", u=2)
                    i = tp[:].rearrange("q (u c) -> q c u", u=2)
                else:
                    o = dst.rearrange("q (g m u) -> q g m u", g=2, u=2)
                    i = tp[:].rearrange("q (g u m) -> q g m u", g=2, u=2)
                if b in V_BANKS[n]:
                    nc.vector.tensor_copy(out=o, in_=i)
                else:
                    nc.scalar.copy(out=o, in_=i)

        def quantise(n, lo, hi):
            nc.vector.quantize_mx(
                out=codes[n][:, 256 * lo : 256 * hi].bitcast(FP8X4),
                scales=planes[n][:, 256 * lo : 256 * hi],
                in_=groups[n][:, 1024 * lo : 1024 * hi],
            )

        vec_w = keep.tile([P, 16], F32, name="vec_w")
        vec_f = keep.tile([P, 32], F32, name="vec_f")
        w0_b = keep.tile([P, E], F32, name="w0_b")

        def vec_prep():
            tpv = ps_pool.tile([P, 512], F32, name="tpv", tag="ps")
            nc.tensor.transpose(tpv[:, 0:128], vec_in[:].bitcast(F32), ident_f[:])
            nc.vector.tensor_copy(out=vec_w[:], in_=tpv[:, 0:16])
            nc.vector.tensor_copy(out=vec_f[:], in_=vec_w[:].bitcast(BF16))

        w0_ps = []

        def w0_mm():
            vb = vec_w[:].bitcast(BF16)
            for half, js in ((0, (0, 1)), (1, (2,))):
                wps = ps_pool.tile([P, 512], F32, name="wps", tag="ps")
                w0_ps.append(wps)
                for jj, j in enumerate(js):
                    for e in range(2):
                        col = 2 * (10 + j) + e
                        nc.tensor.matmul(
                            wps[:, (jj * 2 + e) * 128 : (jj * 2 + e) * 128 + 128],
                            lhsT=vb[:, col : col + 1].to_broadcast([P, P]),
                            rhs=ident_b[:],
                            start=True,
                            stop=True,
                        )

        def w0_out():
            for half, js in ((0, (0, 1)), (1, (2,))):
                wps = w0_ps[half]
                w = 256 * len(js)
                nc.vector.tensor_copy(
                    out=w0_b[:, 512 * half : 512 * half + w].rearrange("c (j p e) -> c j p e", p=128, e=2),
                    in_=wps[:, 0:w].rearrange("c (j e p) -> c j p e", p=128, e=2),
                )

        hbf = [keep.tile([P, 1024], BF16, name="hbf%d" % g) for g in range(2)]
        grp_h = [keep.tile([P, 1024], BF16, name="grp_h%d" % g, align_bytes=64) for g in range(2)]
        codes_h = [keep.tile([P, 256], U32, name="codes_h%d" % g, align_bytes=64) for g in range(2)]
        planes_h = [keep.tile([P, 256], U8, name="planes_h%d" % g, align_bytes=64) for g in range(2)]
        accs = {}

        def mm_hidden(n):
            acc = ps_pool.tile([P, 512], F32, name="acc1", tag="ps")
            acc_b = acc
            if n == 4:
                acc_b = ps_pool.tile([P, 512], F32, name="acc1b", tag="ps")
            accs[n] = (acc, acc_b)
            for e in range(2):
                for g in range(4):
                    cols = slice((e * 4 + g) * 128, (e * 4 + g) * 128 + 128)
                    rc = slice(256 * g, 256 * g + 256)
                    nc.tensor.matmul_mx(
                        out=accs[n][e][:, 256 * e : 256 * e + 256],
                        lhsT=codes[n][:, cols].bitcast(FP8X4),
                        lhsT_scale=planes[n][:, cols],
                        rhs=codes[0][:, rc].bitcast(FP8X4),
                        rhs_scale=planes[0][:, rc],
                        start=(g == 0),
                        stop=(g == 3),
                    )

        def relu_hidden(n):
            a = n - 1
            g2, u2 = a // 2, a % 2
            for e in range(2):
                t = 2 * u2 + e
                if n == 4 and e == 1:
                    nc.vector.tensor_scalar(
                        out=hbf[g2][:, 256 * t : 256 * t + 256],
                        in0=accs[n][e][:, 256 * e : 256 * e + 256],
                        scalar1=vec_f[:, 2 * a + e : 2 * a + e + 1],
                        scalar2=0.0,
                        op0=ALU.add,
                        op1=ALU.max,
                    )
                else:
                    nc.scalar.activation(
                        out=hbf[g2][:, 256 * t : 256 * t + 256],
                        in_=accs[n][e][:, 256 * e : 256 * e + 256],
                        func=ACT.Relu,
                        bias=vec_f[:, 2 * a + e : 2 * a + e + 1],
                    )

        def regroup_hidden(g2):
            nc.vector.tensor_copy(
                out=grp_h[g2][:].rearrange("p (c i t) -> p c t i", i=4, t=4),
                in_=hbf[g2][:].rearrange("p (t c i) -> p c t i", t=4, i=4),
            )

        def quantise_hidden(g2):
            nc.vector.quantize_mx(out=codes_h[g2][:].bitcast(FP8X4), scales=planes_h[g2][:], in_=grp_h[g2][:])

        out_sb = [keep.tile([P, 512], F32, name="out_sb%d" % j) for j in range(3)]
        out_dram = out.rearrange("(a c) x -> c a x", a=2)
        xs = {}

        def mm_out(n, es=(0, 1)):
            if n not in accs:
                acc_g = ps_pool.tile([P, 512], F32, name="acc_g", tag="ps")
                acc_d = ps_pool.tile([P, 512], F32, name="acc_d", tag="ps")
                accs[n] = (acc_d, acc_g)
            for mat in (1, 0):
                for e in es:
                    for g2 in range(2):
                        bank = (1 - mat) * 2 + e
                        cols = slice((bank * 2 + g2) * 128, (bank * 2 + g2) * 128 + 128)
                        nc.tensor.matmul_mx(
                            out=accs[n][mat][:, 256 * e : 256 * e + 256],
                            lhsT=codes[n][:, cols].bitcast(FP8X4),
                            lhsT_scale=planes[n][:, cols],
                            rhs=codes_h[g2][:].bitcast(FP8X4),
                            rhs_scale=planes_h[g2][:],
                            start=(g2 == 0),
                            stop=(g2 == 1),
                        )

        def gate_out(n, es=(0, 1)):
            j = n - 5
            if n not in xs:
                gate = stage.tile([P, 512], F32, name="gate", tag="gate")
                x = stage.tile([P, 512], F32, name="x", tag="x")
                xs[n] = (gate, x)
            gate, x = xs[n]
            acc_d, acc_g = accs[n]
            for e in es:
                cs = slice(256 * e, 256 * e + 256)
                nc.scalar.activation(
                    out=gate[:, cs], in_=acc_g[:, cs], func=ACT.Sigmoid, bias=vec_f[:, 2 * (7 + j) + e : 2 * (7 + j) + e + 1]
                )
            for e in es:
                cs = slice(256 * e, 256 * e + 256)
                nc.vector.scalar_tensor_tensor(
                    out=x[:, cs],
                    in0=acc_d[:, cs],
                    scalar=vec_f[:, 2 * (4 + j) + e : 2 * (4 + j) + e + 1],
                    in1=gate[:, cs],
                    op0=ALU.add,
                    op1=ALU.mult,
                )

        fins = {}

        def back(n):
            x = xs[n][1]
            fin = ps_pool.tile([P, 512], F32, name="fin", tag="ps")
            for a in range(2):
                for e in range(2):
                    nc.tensor.transpose(
                        fin[:, (a * 2 + e) * 128 : (a * 2 + e) * 128 + 128], x[:, 256 * e + 128 * a : 256 * e + 128 * a + 128], ident_f[:]
                    )
            fins[n] = fin

        def finish(n):
            j = n - 5
            xc = slice(256 * j, 256 * j + 256)
            nc.vector.tensor_tensor(
                out=out_sb[j][:].rearrange("c (a p e) -> c a p e", a=2, e=2),
                in0=fins[n][:].rearrange("c (a e p) -> c a p e", a=2, e=2),
                in1=w0_b[:, xc].rearrange("c (p e) -> c p e", e=2).unsqueeze(1).to_broadcast([P, 2, 128, 2]),
                op=ALU.add,
            )
            nc.sync.dma_start(out=out_dram[:, :, xc], in_=out_sb[j][:].rearrange("c (a x) -> c a x", a=2))

        def quantise_all(n):
            quantise(n, 0, 2)
            quantise(n, 2, 4)

        transposes(0)
        empty(0)
        vec_prep()
        transposes(1)
        quantise_all(0)
        empty(1)
        w0_mm()
        transposes(2)
        quantise_all(1)
        w0_out()
        mm_hidden(1)
        empty(2)
        transposes(3)
        quantise_all(2)
        mm_hidden(2)
        relu_hidden(1)
        empty(3)
        transposes(4)
        quantise_all(3)
        mm_hidden(3)
        relu_hidden(2)
        regroup_hidden(0)
        quantise_hidden(0)
        empty(4)
        transposes(5)
        quantise_all(4)
        mm_hidden(4)
        relu_hidden(3)
        empty(5)
        transposes(6)
        quantise_all(5)
        relu_hidden(4)
        regroup_hidden(1)
        quantise_hidden(1)
        empty(6)
        transposes(7)
        quantise_all(6)
        empty(7)
        mm_out(5)
        quantise(7, 0, 2)
        quantise(7, 2, 3)
        quantise(7, 3, 4)
        gate_out(5)
        mm_out(6)
        gate_out(6)
        mm_out(7)
        back(5)
        back(6)
        gate_out(7)
        finish(5)
        back(7)
        finish(6)
        finish(7)
